import numpy as np
import ml_dtypes

BF16 = ml_dtypes.bfloat16


def bf(x):
    return np.asarray(x, np.float32).astype(BF16)


def f32(x):
    return np.asarray(x, np.float32)


def f64(x):
    return np.asarray(x).astype(np.float64)


def striped(idx):
    return np.tile(idx.reshape(-1, 16).T, (8, 1))


C, S, N, HL, DL, HN, UL = 256, 512, 256, 128, 128, 4, 32


def setup_inputs():
    return {"x": f32(0.25 * np.random.standard_normal((C, S))), "bo": f32(0.03 * np.random.standard_normal((C, 1))), "offs": striped(np.random.permutation(np.tile(np.arange(S), 2))[:N])}


def reference(x, bo, offs):
    idx = offs[:16].T.reshape(-1)
    e = f64(x)[:, idx] + f64(bo)
    h = e[:, :HL]
    d = e[:, HL:]
    w = d.T @ h
    a = w.reshape(DL, HN, UL).mean(axis=2)
    p = w * np.repeat(a, UL, axis=1)
    return h @ p.T

@@ -1,0 +1,104 @@
+import concourse.mybir as mybir
+from concourse.masks import make_identity
+
+F32, BF16, U16 = mybir.dt.float32, mybir.dt.bfloat16, mybir.dt.uint16
+ADD, MULT = mybir.AluOpType.add, mybir.AluOpType.mult
+COPY = mybir.ActivationFunctionType.Copy
+
+P = 128
+C, S, N = 256, 512, 256
+HL, DL = 128, 128
+HN, UL = 4, 32
+NB = C // P
+PIECE = 128
+
+WARM_COLUMNS = 512
+WARM_MATMULS = 7
+
+FLOPS = 2 * C * DL * HL + 2 * HL * C * DL
+
+
+def tile_transformerencoderlayer_kernel(tc, x, bo, offs, out):
+    nc = tc.nc
+    with (
+        tc.tile_pool(name="held", bufs=1) as held,
+        tc.psum_pool(name="psum", bufs=1) as psum,
+    ):
+        offsets = held.tile([P, N // 16], U16, name="offsets")
+        nc.sync.dma_start(offsets[:], offs)
+        bias = held.tile([P, NB], F32, name="bias")
+        nc.scalar.dma_start(bias[:], bo.rearrange("(p b) o -> p (b o)", b=NB))
+        x_blocks = x.rearrange("(p b) s -> p b s", b=NB)
+        out_blocks = out.rearrange("(p b) q -> p b q", b=NB)
+        table = [held.tile([P, S], F32, name=f"table{b}") for b in range(NB)]
+        for b in range(NB):
+            nc.sync.dma_start(table[b][0:P:2, :], x_blocks[0:P:2, b, :])
+            nc.scalar.dma_start(table[b][1:P:2, :], x_blocks[1:P:2, b, :])
+
+        identity = held.tile([P, P], BF16, name="identity")
+        make_identity(nc, identity[:])
+
+        warm_in = held.tile([P, WARM_COLUMNS], BF16, name="warm_in")
+        nc.vector.memset(warm_in[:], 0.0)
+        warm_ps = psum.tile([P, WARM_COLUMNS], F32, name="warm_ps")
+        for i in range(WARM_MATMULS):
+            nc.tensor.matmul(warm_ps[:], warm_in[:, 0:P], warm_in[:], start=True, stop=True)
+
+        bias_wide = held.tile([P, NB * PIECE], F32, name="bias_wide")
+        nc.vector.tensor_copy(
+            bias_wide[:].rearrange("p (b j) -> p b j", b=NB), bias[:].unsqueeze(2).to_broadcast([P, NB, PIECE])
+        )
+
+        e32 = [held.tile([P, N], F32, name=f"e32_{b}") for b in range(NB)]
+        e16 = [held.tile([P, N], BF16, name=f"e16_{b}") for b in range(NB)]
+        for b in range(NB):
+            for j in (HL, 0):
+                nc.vector.tensor_tensor(
+                    e32[b][:, j : j + PIECE],
+                    table[b][:].indirect(offsets[:, j // 16 : (j + PIECE) // 16]),
+                    bias_wide[:, b * PIECE : (b + 1) * PIECE],
+                    ADD,
+                )
+                if b == NB - 1 and j == 0:
+                    nc.vector.tensor_copy(e16[b][:, j : j + PIECE], e32[b][:, j : j + PIECE])
+                else:
+                    nc.scalar.activation(e16[b][:, j : j + PIECE], e32[b][:, j : j + PIECE], COPY)
+
+        w_ps = psum.tile([P, HL], F32, name="w_ps")
+        for b in range(NB):
+            nc.tensor.matmul(w_ps[:], e16[b][:, HL:N], e16[b][:, 0:HL], start=(b == 0), stop=(b == NB - 1))
+
+        ht_ps = psum.tile([P, C], BF16, name="ht_ps")
+        for b in range(NB):
+            nc.tensor.transpose(ht_ps[:, b * P : (b + 1) * P], e16[b][:, 0:HL], identity[:])
+        ht = held.tile([P, C], BF16, name="ht")
+        nc.scalar.activation(ht[:], ht_ps[:], COPY)
+
+        w_by_utterance = w_ps[:].rearrange("q (u t) -> q u t", t=UL)
+        a_sum = held.tile([P, HN], F32, name="a_sum")
+        nc.vector.tensor_reduce(a_sum[:], w_by_utterance, mybir.AxisListType.X, ADD)
+        p16 = held.tile([P, HL], BF16, name="p16")
+        nc.vector.scalar_tensor_tensor(
+            p16[:].rearrange("q (u t) -> q u t", t=UL),
+            w_by_utterance,
+            1.0 / UL,
+            a_sum[:].unsqueeze(2).to_broadcast([P, HN, UL]),
+            MULT,
+            MULT,
+        )
+
+        pt_ps = psum.tile([P, DL], BF16, name="pt_ps")
+        nc.tensor.transpose(pt_ps[:], p16[:], identity[:])
+        pt = held.tile([P, DL], BF16, name="pt")
+        nc.vector.tensor_copy(pt[:], pt_ps[:])
+
+        for b in range(NB):
+            o_ps = psum.tile([P, DL], F32, name=f"o_ps{b}")
+            nc.tensor.matmul(o_ps[:], ht[:, b * P : (b + 1) * P], pt[:], start=True, stop=True)
+            o32 = held.tile([P, DL], F32, name=f"o32_{b}")
+            if b == 0:
+                nc.scalar.activation(o32[:], o_ps[:], COPY)
+                nc.scalar.dma_start(out_blocks[:, 0, :], o32[:])
+            else:
+                nc.vector.tensor_copy(o32[:], o_ps[:])
+                nc.sync.dma_start(out_blocks[:, 1, :], o32[:])

@@ -63,6 +63,7 @@ def tile_transformerencoderlayer_kernel(tc, x, bo, offs, out):
                     nc.vector.tensor_copy(e16[b][:, j : j + PIECE], e32[b][:, j : j + PIECE])
                 else:
                     nc.scalar.activation(e16[b][:, j : j + PIECE], e32[b][:, j : j + PIECE], COPY)
+                    nc.tensor.matmul(warm_ps[:], e16[b][:, j : j + PIECE], warm_in[:], start=True, stop=True)
 
         w_ps = psum.tile([P, HL], F32, name="w_ps")
         for b in range(NB):

@@ -63,6 +63,7 @@ def tile_transformerencoderlayer_kernel(tc, x, bo, offs, out):
                     nc.vector.tensor_copy(e16[b][:, j : j + PIECE], e32[b][:, j : j + PIECE])
                 else:
                     nc.scalar.activation(e16[b][:, j : j + PIECE], e32[b][:, j : j + PIECE], COPY)
+                if b == 0:
                     nc.tensor.matmul(warm_ps[:], e16[b][:, j : j + PIECE], warm_in[:], start=True, stop=True)
 
         w_ps = psum.tile([P, HL], F32, name="w_ps")

@@ -72,7 +72,7 @@ def tile_transformerencoderlayer_kernel(tc, x, bo, offs, out):
 
         ht_ps = psum.tile([P, C], BF16, name="ht_ps")
         for b in range(NB):
-            nc.tensor.transpose(ht_ps[:, b * P : (b + 1) * P], e16[b][:, 0:HL], identity[:])
+            nc.tensor.matmul(ht_ps[:, b * P : (b + 1) * P], e16[b][:, 0:HL], identity[:], start=True, stop=True)
         ht = held.tile([P, C], BF16, name="ht")
         nc.scalar.activation(ht[:], ht_ps[:], COPY)
 
@@ -90,7 +90,7 @@ def tile_transformerencoderlayer_kernel(tc, x, bo, offs, out):
         )
 
         pt_ps = psum.tile([P, DL], BF16, name="pt_ps")
-        nc.tensor.transpose(pt_ps[:], p16[:], identity[:])
+        nc.tensor.matmul(pt_ps[:], p16[:], identity[:], start=True, stop=True)
         pt = held.tile([P, DL], BF16, name="pt")
         nc.vector.tensor_copy(pt[:], pt_ps[:])
 

@@ -11,6 +11,7 @@ HL, DL = 128, 128
 HN, UL = 4, 32
 NB = C // P
 PIECE = 128
+DMA_ROW_ALIGN = 256
 
 WARM_COLUMNS = 512
 WARM_MATMULS = 7
@@ -30,7 +31,7 @@ def tile_transformerencoderlayer_kernel(tc, x, bo, offs, out):
         nc.scalar.dma_start(bias[:], bo.rearrange("(p b) o -> p (b o)", b=NB))
         x_blocks = x.rearrange("(p b) s -> p b s", b=NB)
         out_blocks = out.rearrange("(p b) q -> p b q", b=NB)
-        table = [held.tile([P, S], F32, name=f"table{b}") for b in range(NB)]
+        table = [held.tile([P, S], F32, name=f"table{b}", align_bytes=DMA_ROW_ALIGN) for b in range(NB)]
         for b in range(NB):
             nc.sync.dma_start(table[b][0:P:2, :], x_blocks[0:P:2, b, :])
             nc.scalar.dma_start(table[b][1:P:2, :], x_blocks[1:P:2, b, :])
@@ -97,7 +98,7 @@ def tile_transformerencoderlayer_kernel(tc, x, bo, offs, out):
         for b in range(NB):
             o_ps = psum.tile([P, DL], F32, name=f"o_ps{b}")
             nc.tensor.matmul(o_ps[:], ht[:, b * P : (b + 1) * P], pt[:], start=True, stop=True)
-            o32 = held.tile([P, DL], F32, name=f"o32_{b}")
+            o32 = held.tile([P, DL], F32, name=f"o32_{b}", align_bytes=DMA_ROW_ALIGN)
             if b == 0:
                 nc.scalar.activation(o32[:], o_ps[:], COPY)
                 nc.scalar.dma_start(out_blocks[:, 0, :], o32[:])

@@ -25,9 +25,9 @@ def tile_transformerencoderlayer_kernel(tc, x, bo, offs, out):
         tc.tile_pool(name="held", bufs=1) as held,
         tc.psum_pool(name="psum", bufs=1) as psum,
     ):
-        offsets = held.tile([P, N // 16], U16, name="offsets")
+        offsets = held.tile([P, N // 16], U16, name="offsets", align_bytes=DMA_ROW_ALIGN)
         nc.sync.dma_start(offsets[:], offs)
-        bias = held.tile([P, NB], F32, name="bias")
+        bias = held.tile([P, NB], F32, name="bias", align_bytes=DMA_ROW_ALIGN)
         nc.scalar.dma_start(bias[:], bo.rearrange("(p b) o -> p (b o)", b=NB))
         x_blocks = x.rearrange("(p b) s -> p b s", b=NB)
         out_blocks = out.rearrange("(p b) q -> p b q", b=NB)

import concourse.mybir as mybir
from concourse.masks import make_identity

F32, BF16, U16 = mybir.dt.float32, mybir.dt.bfloat16, mybir.dt.uint16
ADD, MULT = mybir.AluOpType.add, mybir.AluOpType.mult
COPY = mybir.ActivationFunctionType.Copy

P = 128
C, S, N = 256, 512, 256
HL, DL = 128, 128
HN, UL = 4, 32
NB = C // P
PIECE = 128
DMA_ROW_ALIGN = 256

WARM_COLUMNS = 512
WARM_MATMULS = 7

FLOPS = 2 * C * DL * HL + 2 * HL * C * DL


def tile_transformerencoderlayer_kernel(tc, x, bo, offs, out):
    nc = tc.nc
    with (
        tc.tile_pool(name="held", bufs=1) as held,
        tc.psum_pool(name="psum", bufs=1) as psum,
    ):
        offsets = held.tile([P, N // 16], U16, name="offsets", align_bytes=DMA_ROW_ALIGN)
        nc.sync.dma_start(offsets[:], offs)
        bias = held.tile([P, NB], F32, name="bias", align_bytes=DMA_ROW_ALIGN)
        nc.scalar.dma_start(bias[:], bo.rearrange("(p b) o -> p (b o)", b=NB))
        x_blocks = x.rearrange("(p b) s -> p b s", b=NB)
        out_blocks = out.rearrange("(p b) q -> p b q", b=NB)
        table = [held.tile([P, S], F32, name=f"table{b}", align_bytes=DMA_ROW_ALIGN) for b in range(NB)]
        for b in range(NB):
            nc.sync.dma_start(table[b][0:P:2, :], x_blocks[0:P:2, b, :])
            nc.scalar.dma_start(table[b][1:P:2, :], x_blocks[1:P:2, b, :])

        identity = held.tile([P, P], BF16, name="identity")
        make_identity(nc, identity[:])

        warm_in = held.tile([P, WARM_COLUMNS], BF16, name="warm_in")
        nc.vector.memset(warm_in[:], 0.0)
        warm_ps = psum.tile([P, WARM_COLUMNS], F32, name="warm_ps")
        for i in range(WARM_MATMULS):
            nc.tensor.matmul(warm_ps[:], warm_in[:, 0:P], warm_in[:], start=True, stop=True)

        bias_wide = held.tile([P, NB * PIECE], F32, name="bias_wide")
        nc.vector.tensor_copy(
            bias_wide[:].rearrange("p (b j) -> p b j", b=NB), bias[:].unsqueeze(2).to_broadcast([P, NB, PIECE])
        )

        e32 = [held.tile([P, N], F32, name=f"e32_{b}") for b in range(NB)]
        e16 = [held.tile([P, N], BF16, name=f"e16_{b}") for b in range(NB)]
        for b in range(NB):
            for j in (HL, 0):
                nc.vector.tensor_tensor(
                    e32[b][:, j : j + PIECE],
                    table[b][:].indirect(offsets[:, j // 16 : (j + PIECE) // 16]),
                    bias_wide[:, b * PIECE : (b + 1) * PIECE],
                    ADD,
                )
                if b == NB - 1 and j == 0:
                    nc.vector.tensor_copy(e16[b][:, j : j + PIECE], e32[b][:, j : j + PIECE])
                else:
                    nc.scalar.activation(e16[b][:, j : j + PIECE], e32[b][:, j : j + PIECE], COPY)
                if b == 0:
                    nc.tensor.matmul(warm_ps[:], e16[b][:, j : j + PIECE], warm_in[:], start=True, stop=True)

        w_ps = psum.tile([P, HL], F32, name="w_ps")
        for b in range(NB):
            nc.tensor.matmul(w_ps[:], e16[b][:, HL:N], e16[b][:, 0:HL], start=(b == 0), stop=(b == NB - 1))

        ht_ps = psum.tile([P, C], BF16, name="ht_ps")
        for b in range(NB):
            nc.tensor.matmul(ht_ps[:, b * P : (b + 1) * P], e16[b][:, 0:HL], identity[:], start=True, stop=True)
        ht = held.tile([P, C], BF16, name="ht")
        nc.scalar.activation(ht[:], ht_ps[:], COPY)

        w_by_utterance = w_ps[:].rearrange("q (u t) -> q u t", t=UL)
        a_sum = held.tile([P, HN], F32, name="a_sum")
        nc.vector.tensor_reduce(a_sum[:], w_by_utterance, mybir.AxisListType.X, ADD)
        p16 = held.tile([P, HL], BF16, name="p16")
        nc.vector.scalar_tensor_tensor(
            p16[:].rearrange("q (u t) -> q u t", t=UL),
            w_by_utterance,
            1.0 / UL,
            a_sum[:].unsqueeze(2).to_broadcast([P, HN, UL]),
            MULT,
            MULT,
        )

        pt_ps = psum.tile([P, DL], BF16, name="pt_ps")
        nc.tensor.matmul(pt_ps[:], p16[:], identity[:], start=True, stop=True)
        pt = held.tile([P, DL], BF16, name="pt")
        nc.vector.tensor_copy(pt[:], pt_ps[:])

        for b in range(NB):
            o_ps = psum.tile([P, DL], F32, name=f"o_ps{b}")
            nc.tensor.matmul(o_ps[:], ht[:, b * P : (b + 1) * P], pt[:], start=True, stop=True)
            o32 = held.tile([P, DL], F32, name=f"o32_{b}", align_bytes=DMA_ROW_ALIGN)
            if b == 0:
                nc.scalar.activation(o32[:], o_ps[:], COPY)
                nc.scalar.dma_start(out_blocks[:, 0, :], o32[:])
            else:
                nc.vector.tensor_copy(o32[:], o_ps[:])
                nc.sync.dma_start(out_blocks[:, 1, :], o32[:])
